import numpy as np
import ml_dtypes

BF16 = ml_dtypes.bfloat16


def bf(x):
    return np.asarray(x, np.float32).astype(BF16)


def f32(x):
    return np.asarray(x, np.float32)


def f64(x):
    return np.asarray(x).astype(np.float64)


def striped(idx):
    return np.tile(idx.reshape(-1, 16).T, (8, 1))


C, S, N = 512, 4096, 512
SCALE = np.sqrt(C)
EPS = 1e-5


def setup_inputs():
    return {"emb": f32(0.05 * np.random.standard_normal((C, S))), "pos": f32(0.5 * np.random.standard_normal((C, N))), "ln_emb_s": f32(1.0 + 0.1 * np.random.standard_normal((C, 1))), "ln_emb_b": f32(0.1 * np.random.standard_normal((C, 1))), "offs": striped(np.random.permutation(np.tile(np.arange(S), 2))[:N])}


def reference(emb, pos, ln_emb_s, ln_emb_b, offs):
    idx = offs[:16].T.reshape(-1)
    xs = SCALE * f64(emb)
    h = xs[:, idx] + f64(pos)
    mu = h.mean(axis=0, keepdims=True)
    d = h - mu
    var = (d * d).mean(axis=0, keepdims=True)
    return d / np.sqrt(var + EPS) * f64(ln_emb_s) + f64(ln_emb_b)

@@ -1,0 +1,83 @@
+import math
+
+import concourse.mybir as mybir
+
+P = 128
+C, S, N = 512, 4096, 512
+BLOCKS = C // P
+CHUNK = 1024
+EPS = 1e-5
+FLOPS = C * S + 8 * C * N
+
+F32 = mybir.dt.float32
+U16 = mybir.dt.uint16
+ALU = mybir.AluOpType
+ACT = mybir.ActivationFunctionType
+
+
+def tile_blockdiffusiondecoder_kernel(tc, emb, pos, ln_emb_s, ln_emb_b, offs, out):
+    nc = tc.nc
+    with (
+        tc.tile_pool(name="held", bufs=1) as held,
+        tc.tile_pool(name="raw_ring", bufs=8) as raw_ring,
+        tc.tile_pool(name="work", bufs=2) as work,
+        tc.psum_pool(name="psum", bufs=1) as psum,
+    ):
+        offsets = held.tile([P, N // 16], U16, name="offsets")
+        nc.sync.dma_start(offsets[:], offs)
+
+        gain = held.tile([P, BLOCKS], F32, name="gain")
+        bias = held.tile([P, BLOCKS], F32, name="bias")
+        with nc.allow_non_contiguous_dma(reason="512 gains and biases, one to a partition"):
+            nc.scalar.dma_start(gain[:], ln_emb_s.rearrange("(b p) o -> p (b o)", p=P))
+            nc.scalar.dma_start(bias[:], ln_emb_b.rearrange("(b p) o -> p (b o)", p=P))
+
+        mean_w = held.tile([P, P], F32, name="mean_w")
+        nc.gpsimd.memset(mean_w[:], 1.0 / C)
+        eps = held.tile([P, 1], F32, name="eps")
+        nc.gpsimd.memset(eps[:], EPS)
+
+        mean_ps = psum.tile([P, N], F32, name="mean_ps")
+        var_ps = psum.tile([P, N], F32, name="var_ps")
+
+        h = []
+        for b in range(BLOCKS):
+            rows = slice(b * P, (b + 1) * P)
+            pos_b = held.tile([P, N], F32, name=f"pos{b}")
+            nc.sync.dma_start(pos_b[:], pos[rows, :])
+            xs_b = held.tile([P, S], F32, name=f"xs{b}")
+            for k in range(S // CHUNK):
+                cols = slice(k * CHUNK, (k + 1) * CHUNK)
+                raw = raw_ring.tile([P, CHUNK], F32, name="raw")
+                nc.sync.dma_start(raw[:], emb[rows, cols])
+                if k % 2 == 0:
+                    nc.vector.tensor_scalar_mul(xs_b[:, cols], raw[:], math.sqrt(C))
+                else:
+                    nc.scalar.mul(xs_b[:, cols], raw[:], math.sqrt(C))
+            h_b = held.tile([P, N], F32, name=f"h{b}")
+            nc.vector.tensor_tensor(h_b[:], xs_b[:].indirect(offsets[:]), pos_b[:], ALU.add)
+            nc.tensor.matmul(mean_ps[:], mean_w[:], h_b[:], start=(b == 0), stop=(b == BLOCKS - 1))
+            h.append(h_b)
+
+        d = []
+        for b in range(BLOCKS):
+            d_b = held.tile([P, N], F32, name=f"d{b}")
+            nc.vector.tensor_tensor(d_b[:], h[b][:], mean_ps[:], ALU.subtract)
+            sq = work.tile([P, N], F32, name="sq")
+            nc.scalar.square(sq[:], d_b[:])
+            nc.tensor.matmul(var_ps[:], mean_w[:], sq[:], start=(b == 0), stop=(b == BLOCKS - 1))
+            d.append(d_b)
+
+        std = held.tile([P, N], F32, name="std")
+        nc.scalar.activation(std[:], var_ps[:], ACT.Sqrt, bias=eps[:])
+        rstd = held.tile([P, N], F32, name="rstd")
+        nc.vector.reciprocal(rstd[:], std[:])
+
+        for b in range(BLOCKS):
+            normed = work.tile([P, N], F32, name="normed")
+            nc.vector.tensor_tensor(normed[:], d[b][:], rstd[:], ALU.mult)
+            out_b = work.tile([P, N], F32, name="out_b")
+            nc.scalar.activation(
+                out_b[:], normed[:], ACT.Identity, bias=bias[:, b : b + 1], scale=gain[:, b : b + 1]
+            )
+            nc.sync.dma_start(out[b * P : (b + 1) * P, :], out_b[:])

@@ -68,10 +68,8 @@ def tile_blockdiffusiondecoder_kernel(tc, emb, pos, ln_emb_s, ln_emb_b, offs, ou
             nc.tensor.matmul(var_ps[:], mean_w[:], sq[:], start=(b == 0), stop=(b == BLOCKS - 1))
             d.append(d_b)
 
-        std = held.tile([P, N], F32, name="std")
-        nc.scalar.activation(std[:], var_ps[:], ACT.Sqrt, bias=eps[:])
         rstd = held.tile([P, N], F32, name="rstd")
-        nc.vector.reciprocal(rstd[:], std[:])
+        nc.scalar.activation(rstd[:], var_ps[:], ACT.Abs_reciprocal_sqrt, bias=eps[:])
 
         for b in range(BLOCKS):
             normed = work.tile([P, N], F32, name="normed")

@@ -32,15 +32,21 @@ def tile_blockdiffusiondecoder_kernel(tc, emb, pos, ln_emb_s, ln_emb_b, offs, ou
             nc.scalar.dma_start(gain[:], ln_emb_s.rearrange("(b p) o -> p (b o)", p=P))
             nc.scalar.dma_start(bias[:], ln_emb_b.rearrange("(b p) o -> p (b o)", p=P))
 
+        block_mean_w = held.tile([P, P], F32, name="block_mean_w")
+        nc.gpsimd.memset(block_mean_w[:], 1.0 / P)
         mean_w = held.tile([P, P], F32, name="mean_w")
         nc.gpsimd.memset(mean_w[:], 1.0 / C)
         eps = held.tile([P, 1], F32, name="eps")
         nc.gpsimd.memset(eps[:], EPS)
 
-        mean_ps = psum.tile([P, N], F32, name="mean_ps")
-        var_ps = psum.tile([P, N], F32, name="var_ps")
+        warm = held.tile([P, 1], F32, name="warm")
+        nc.scalar.activation(warm[:], eps[:], ACT.Abs_reciprocal_sqrt)
 
-        h = []
+        pivot_ps = psum.tile([P, N], F32, name="pivot_ps")
+        m_ps = psum.tile([P, N], F32, name="m_ps")
+        q_ps = psum.tile([P, N], F32, name="q_ps")
+
+        d = []
         for b in range(BLOCKS):
             rows = slice(b * P, (b + 1) * P)
             pos_b = held.tile([P, N], F32, name=f"pos{b}")
@@ -54,26 +60,42 @@ def tile_blockdiffusiondecoder_kernel(tc, emb, pos, ln_emb_s, ln_emb_b, offs, ou
                     nc.vector.tensor_scalar_mul(xs_b[:, cols], raw[:], math.sqrt(C))
                 else:
                     nc.scalar.mul(xs_b[:, cols], raw[:], math.sqrt(C))
-            h_b = held.tile([P, N], F32, name=f"h{b}")
-            nc.vector.tensor_tensor(h_b[:], xs_b[:].indirect(offsets[:]), pos_b[:], ALU.add)
-            nc.tensor.matmul(mean_ps[:], mean_w[:], h_b[:], start=(b == 0), stop=(b == BLOCKS - 1))
-            h.append(h_b)
 
-        d = []
-        for b in range(BLOCKS):
             d_b = held.tile([P, N], F32, name=f"d{b}")
-            nc.vector.tensor_tensor(d_b[:], h[b][:], mean_ps[:], ALU.subtract)
-            sq = work.tile([P, N], F32, name="sq")
-            nc.scalar.square(sq[:], d_b[:])
-            nc.tensor.matmul(var_ps[:], mean_w[:], sq[:], start=(b == 0), stop=(b == BLOCKS - 1))
+            if b == 0:
+                h0 = held.tile([P, N], F32, name="h0")
+                nc.vector.tensor_tensor(h0[:], xs_b[:].indirect(offsets[:]), pos_b[:], ALU.add)
+                nc.tensor.matmul(pivot_ps[:], block_mean_w[:], h0[:], start=True, stop=True)
+                nc.vector.tensor_tensor(d_b[:], h0[:], pivot_ps[:], ALU.subtract)
+            else:
+                shifted = held.tile([P, N], F32, name=f"shifted{b}")
+                nc.vector.tensor_tensor(shifted[:], pos_b[:], pivot_ps[:], ALU.subtract)
+                nc.vector.tensor_tensor(d_b[:], xs_b[:].indirect(offsets[:]), shifted[:], ALU.add)
             d.append(d_b)
 
+            sq = work.tile([P, N], F32, name="sq")
+            nc.scalar.square(sq[:], d_b[:])
+            nc.tensor.matmul(m_ps[:], mean_w[:], d_b[:], start=(b == 0), stop=(b == BLOCKS - 1))
+            nc.tensor.matmul(q_ps[:], mean_w[:], sq[:], start=(b == 0), stop=(b == BLOCKS - 1))
+
+        m = held.tile([P, N], F32, name="m")
+        nc.scalar.copy(m[:], m_ps[:])
+        m_squared = held.tile([P, N], F32, name="m_squared")
+        nc.scalar.square(m_squared[:], m_ps[:])
+        var = held.tile([P, N], F32, name="var")
+        nc.vector.tensor_tensor(var[:], q_ps[:], m_squared[:], ALU.subtract)
         rstd = held.tile([P, N], F32, name="rstd")
-        nc.scalar.activation(rstd[:], var_ps[:], ACT.Abs_reciprocal_sqrt, bias=eps[:])
+        nc.scalar.activation(rstd[:], var[:], ACT.Abs_reciprocal_sqrt, bias=eps[:])
+
+        centred = []
+        for b in range(BLOCKS):
+            centred_b = held.tile([P, N], F32, name=f"centred{b}")
+            nc.vector.tensor_tensor(centred_b[:], d[b][:], m[:], ALU.subtract)
+            centred.append(centred_b)
 
         for b in range(BLOCKS):
             normed = work.tile([P, N], F32, name="normed")
-            nc.vector.tensor_tensor(normed[:], d[b][:], rstd[:], ALU.mult)
+            nc.vector.tensor_tensor(normed[:], centred[b][:], rstd[:], ALU.mult)
             out_b = work.tile([P, N], F32, name="out_b")
             nc.scalar.activation(
                 out_b[:], normed[:], ACT.Identity, bias=bias[:, b : b + 1], scale=gain[:, b : b + 1]

@@ -6,6 +6,7 @@ P = 128
 C, S, N = 512, 4096, 512
 BLOCKS = C // P
 CHUNK = 1024
+VECTOR_COLS = 2 * CHUNK // 3 // 8 * 8
 EPS = 1e-5
 FLOPS = C * S + 8 * C * N
 
@@ -20,7 +21,6 @@ def tile_blockdiffusiondecoder_kernel(tc, emb, pos, ln_emb_s, ln_emb_b, offs, ou
     with (
         tc.tile_pool(name="held", bufs=1) as held,
         tc.tile_pool(name="raw_ring", bufs=8) as raw_ring,
-        tc.tile_pool(name="work", bufs=2) as work,
         tc.psum_pool(name="psum", bufs=1) as psum,
     ):
         offsets = held.tile([P, N // 16], U16, name="offsets")
@@ -53,13 +53,13 @@ def tile_blockdiffusiondecoder_kernel(tc, emb, pos, ln_emb_s, ln_emb_b, offs, ou
             nc.sync.dma_start(pos_b[:], pos[rows, :])
             xs_b = held.tile([P, S], F32, name=f"xs{b}")
             for k in range(S // CHUNK):
-                cols = slice(k * CHUNK, (k + 1) * CHUNK)
                 raw = raw_ring.tile([P, CHUNK], F32, name="raw")
-                nc.sync.dma_start(raw[:], emb[rows, cols])
-                if k % 2 == 0:
-                    nc.vector.tensor_scalar_mul(xs_b[:, cols], raw[:], math.sqrt(C))
-                else:
-                    nc.scalar.mul(xs_b[:, cols], raw[:], math.sqrt(C))
+                nc.sync.dma_start(raw[:], emb[rows, k * CHUNK : (k + 1) * CHUNK])
+                xs_chunk = xs_b[:, k * CHUNK : (k + 1) * CHUNK]
+                nc.vector.tensor_scalar_mul(
+                    xs_chunk[:, :VECTOR_COLS], raw[:, :VECTOR_COLS], math.sqrt(C)
+                )
+                nc.scalar.mul(xs_chunk[:, VECTOR_COLS:], raw[:, VECTOR_COLS:], math.sqrt(C))
 
             d_b = held.tile([P, N], F32, name=f"d{b}")
             if b == 0:
@@ -73,7 +73,7 @@ def tile_blockdiffusiondecoder_kernel(tc, emb, pos, ln_emb_s, ln_emb_b, offs, ou
                 nc.vector.tensor_tensor(d_b[:], xs_b[:].indirect(offsets[:]), shifted[:], ALU.add)
             d.append(d_b)
 
-            sq = work.tile([P, N], F32, name="sq")
+            sq = held.tile([P, N], F32, name=f"sq{b}")
             nc.scalar.square(sq[:], d_b[:])
             nc.tensor.matmul(m_ps[:], mean_w[:], d_b[:], start=(b == 0), stop=(b == BLOCKS - 1))
             nc.tensor.matmul(q_ps[:], mean_w[:], sq[:], start=(b == 0), stop=(b == BLOCKS - 1))
@@ -94,9 +94,9 @@ def tile_blockdiffusiondecoder_kernel(tc, emb, pos, ln_emb_s, ln_emb_b, offs, ou
             centred.append(centred_b)
 
         for b in range(BLOCKS):
-            normed = work.tile([P, N], F32, name="normed")
+            normed = held.tile([P, N], F32, name=f"normed{b}")
             nc.vector.tensor_tensor(normed[:], centred[b][:], rstd[:], ALU.mult)
-            out_b = work.tile([P, N], F32, name="out_b")
+            out_b = held.tile([P, N], F32, name=f"out{b}")
             nc.scalar.activation(
                 out_b[:], normed[:], ACT.Identity, bias=bias[:, b : b + 1], scale=gain[:, b : b + 1]
             )

@@ -7,6 +7,8 @@ C, S, N = 512, 4096, 512
 BLOCKS = C // P
 CHUNK = 1024
 VECTOR_COLS = 2 * CHUNK // 3 // 8 * 8
+PIECES = 2
+M = N // PIECES
 EPS = 1e-5
 FLOPS = C * S + 8 * C * N
 
@@ -42,11 +44,11 @@ def tile_blockdiffusiondecoder_kernel(tc, emb, pos, ln_emb_s, ln_emb_b, offs, ou
         warm = held.tile([P, 1], F32, name="warm")
         nc.scalar.activation(warm[:], eps[:], ACT.Abs_reciprocal_sqrt)
 
-        pivot_ps = psum.tile([P, N], F32, name="pivot_ps")
-        m_ps = psum.tile([P, N], F32, name="m_ps")
-        q_ps = psum.tile([P, N], F32, name="q_ps")
+        pivot_ps = [psum.tile([P, M], F32, name=f"pivot_ps{t}") for t in range(PIECES)]
+        m_ps = [psum.tile([P, M], F32, name=f"m_ps{t}") for t in range(PIECES)]
+        q_ps = [psum.tile([P, M], F32, name=f"q_ps{t}") for t in range(PIECES)]
 
-        d = []
+        d = {}
         for b in range(BLOCKS):
             rows = slice(b * P, (b + 1) * P)
             pos_b = held.tile([P, N], F32, name=f"pos{b}")
@@ -61,43 +63,53 @@ def tile_blockdiffusiondecoder_kernel(tc, emb, pos, ln_emb_s, ln_emb_b, offs, ou
                 )
                 nc.scalar.mul(xs_chunk[:, VECTOR_COLS:], raw[:, VECTOR_COLS:], math.sqrt(C))
 
-            d_b = held.tile([P, N], F32, name=f"d{b}")
-            if b == 0:
-                h0 = held.tile([P, N], F32, name="h0")
-                nc.vector.tensor_tensor(h0[:], xs_b[:].indirect(offsets[:]), pos_b[:], ALU.add)
-                nc.tensor.matmul(pivot_ps[:], block_mean_w[:], h0[:], start=True, stop=True)
-                nc.vector.tensor_tensor(d_b[:], h0[:], pivot_ps[:], ALU.subtract)
-            else:
-                shifted = held.tile([P, N], F32, name=f"shifted{b}")
-                nc.vector.tensor_tensor(shifted[:], pos_b[:], pivot_ps[:], ALU.subtract)
-                nc.vector.tensor_tensor(d_b[:], xs_b[:].indirect(offsets[:]), shifted[:], ALU.add)
-            d.append(d_b)
+            first, last = b == 0, b == BLOCKS - 1
+            for t in range(PIECES):
+                looked_up = xs_b[:].indirect(offsets[:, t * (M // 16) : (t + 1) * (M // 16)])
+                pos_piece = pos_b[:, t * M : (t + 1) * M]
+                d[b, t] = held.tile([P, M], F32, name=f"d{b}_{t}")
+                if first:
+                    h0 = held.tile([P, M], F32, name=f"h0_{t}")
+                    nc.vector.tensor_tensor(h0[:], looked_up, pos_piece, ALU.add)
+                    nc.tensor.matmul(pivot_ps[t][:], block_mean_w[:], h0[:], start=True, stop=True)
+                    nc.vector.tensor_tensor(d[b, t][:], h0[:], pivot_ps[t][:], ALU.subtract)
+                else:
+                    shifted = held.tile([P, M], F32, name=f"shifted{b}_{t}")
+                    nc.vector.tensor_tensor(shifted[:], pos_piece, pivot_ps[t][:], ALU.subtract)
+                    nc.vector.tensor_tensor(d[b, t][:], looked_up, shifted[:], ALU.add)
+                sq = held.tile([P, M], F32, name=f"sq{b}_{t}")
+                nc.scalar.square(sq[:], d[b, t][:])
+                nc.tensor.matmul(m_ps[t][:], mean_w[:], d[b, t][:], start=first, stop=last)
+                nc.tensor.matmul(q_ps[t][:], mean_w[:], sq[:], start=first, stop=last)
 
-            sq = held.tile([P, N], F32, name=f"sq{b}")
-            nc.scalar.square(sq[:], d_b[:])
-            nc.tensor.matmul(m_ps[:], mean_w[:], d_b[:], start=(b == 0), stop=(b == BLOCKS - 1))
-            nc.tensor.matmul(q_ps[:], mean_w[:], sq[:], start=(b == 0), stop=(b == BLOCKS - 1))
+        m, rstd = [], []
+        for t in range(PIECES):
+            m_t = held.tile([P, M], F32, name=f"m{t}")
+            nc.scalar.copy(m_t[:], m_ps[t][:])
+            m_squared = held.tile([P, M], F32, name=f"m_squared{t}")
+            nc.scalar.square(m_squared[:], m_ps[t][:])
+            var = held.tile([P, M], F32, name=f"var{t}")
+            nc.vector.tensor_tensor(var[:], q_ps[t][:], m_squared[:], ALU.subtract)
+            rstd_t = held.tile([P, M], F32, name=f"rstd{t}")
+            nc.scalar.activation(rstd_t[:], var[:], ACT.Abs_reciprocal_sqrt, bias=eps[:])
+            m.append(m_t)
+            rstd.append(rstd_t)
 
-        m = held.tile([P, N], F32, name="m")
-        nc.scalar.copy(m[:], m_ps[:])
-        m_squared = held.tile([P, N], F32, name="m_squared")
-        nc.scalar.square(m_squared[:], m_ps[:])
-        var = held.tile([P, N], F32, name="var")
-        nc.vector.tensor_tensor(var[:], q_ps[:], m_squared[:], ALU.subtract)
-        rstd = held.tile([P, N], F32, name="rstd")
-        nc.scalar.activation(rstd[:], var[:], ACT.Abs_reciprocal_sqrt, bias=eps[:])
-
-        centred = []
-        for b in range(BLOCKS):
-            centred_b = held.tile([P, N], F32, name=f"centred{b}")
-            nc.vector.tensor_tensor(centred_b[:], d[b][:], m[:], ALU.subtract)
-            centred.append(centred_b)
-
-        for b in range(BLOCKS):
-            normed = held.tile([P, N], F32, name=f"normed{b}")
-            nc.vector.tensor_tensor(normed[:], centred[b][:], rstd[:], ALU.mult)
-            out_b = held.tile([P, N], F32, name=f"out{b}")
-            nc.scalar.activation(
-                out_b[:], normed[:], ACT.Identity, bias=bias[:, b : b + 1], scale=gain[:, b : b + 1]
-            )
-            nc.sync.dma_start(out[b * P : (b + 1) * P, :], out_b[:])
+        for t in range(PIECES):
+            centred = []
+            for b in range(BLOCKS):
+                centred_b = held.tile([P, M], F32, name=f"centred{b}_{t}")
+                nc.vector.tensor_tensor(centred_b[:], d[b, t][:], m[t][:], ALU.subtract)
+                centred.append(centred_b)
+            for b in range(BLOCKS):
+                normed = held.tile([P, M], F32, name=f"normed{b}_{t}")
+                nc.vector.tensor_tensor(normed[:], centred[b][:], rstd[t][:], ALU.mult)
+                out_piece = held.tile([P, M], F32, name=f"out{b}_{t}")
+                nc.scalar.activation(
+                    out_piece[:],
+                    normed[:],
+                    ACT.Identity,
+                    bias=bias[:, b : b + 1],
+                    scale=gain[:, b : b + 1],
+                )
+                nc.sync.dma_start(out[b * P : (b + 1) * P, t * M : (t + 1) * M], out_piece[:])

@@ -1,12 +1,11 @@
 import math
 
 import concourse.mybir as mybir
+from concourse.masks import make_identity
 
 P = 128
 C, S, N = 512, 4096, 512
 BLOCKS = C // P
-CHUNK = 1024
-VECTOR_COLS = 2 * CHUNK // 3 // 8 * 8
 PIECES = 2
 M = N // PIECES
 EPS = 1e-5
@@ -18,21 +17,30 @@ ALU = mybir.AluOpType
 ACT = mybir.ActivationFunctionType
 
 
+def load_widths(b):
+    if b < BLOCKS - 1:
+        return [S]
+    return [S // 2, S // 4, S // 8, S // 8]
+
+
 def tile_blockdiffusiondecoder_kernel(tc, emb, pos, ln_emb_s, ln_emb_b, offs, out):
     nc = tc.nc
     with (
         tc.tile_pool(name="held", bufs=1) as held,
-        tc.tile_pool(name="raw_ring", bufs=8) as raw_ring,
         tc.psum_pool(name="psum", bufs=1) as psum,
     ):
         offsets = held.tile([P, N // 16], U16, name="offsets")
         nc.sync.dma_start(offsets[:], offs)
 
-        gain = held.tile([P, BLOCKS], F32, name="gain")
-        bias = held.tile([P, BLOCKS], F32, name="bias")
-        with nc.allow_non_contiguous_dma(reason="512 gains and biases, one to a partition"):
-            nc.scalar.dma_start(gain[:], ln_emb_s.rearrange("(b p) o -> p (b o)", p=P))
-            nc.scalar.dma_start(bias[:], ln_emb_b.rearrange("(b p) o -> p (b o)", p=P))
+        rows = held.tile([2 * BLOCKS, P], F32, name="rows")
+        nc.scalar.dma_start(rows[:BLOCKS, :], ln_emb_s.rearrange("(b p) o -> b (p o)", p=P))
+        nc.scalar.dma_start(rows[BLOCKS:, :], ln_emb_b.rearrange("(b p) o -> b (p o)", p=P))
+        identity = held.tile([2 * BLOCKS, 2 * BLOCKS], F32, name="identity")
+        make_identity(nc, identity[:])
+        gain_bias_ps = psum.tile([P, 2 * BLOCKS], F32, name="gain_bias_ps")
+        nc.tensor.matmul(gain_bias_ps[:], rows[:], identity[:], start=True, stop=True)
+        gain_bias = held.tile([P, 2 * BLOCKS], F32, name="gain_bias")
+        nc.vector.tensor_copy(gain_bias[:], gain_bias_ps[:])
 
         block_mean_w = held.tile([P, P], F32, name="block_mean_w")
         nc.gpsimd.memset(block_mean_w[:], 1.0 / P)
@@ -50,18 +58,19 @@ def tile_blockdiffusiondecoder_kernel(tc, emb, pos, ln_emb_s, ln_emb_b, offs, ou
 
         d = {}
         for b in range(BLOCKS):
-            rows = slice(b * P, (b + 1) * P)
+            channels = slice(b * P, (b + 1) * P)
             pos_b = held.tile([P, N], F32, name=f"pos{b}")
-            nc.sync.dma_start(pos_b[:], pos[rows, :])
+            nc.sync.dma_start(pos_b[:], pos[channels, :])
+
             xs_b = held.tile([P, S], F32, name=f"xs{b}")
-            for k in range(S // CHUNK):
-                raw = raw_ring.tile([P, CHUNK], F32, name="raw")
-                nc.sync.dma_start(raw[:], emb[rows, k * CHUNK : (k + 1) * CHUNK])
-                xs_chunk = xs_b[:, k * CHUNK : (k + 1) * CHUNK]
-                nc.vector.tensor_scalar_mul(
-                    xs_chunk[:, :VECTOR_COLS], raw[:, :VECTOR_COLS], math.sqrt(C)
-                )
-                nc.scalar.mul(xs_chunk[:, VECTOR_COLS:], raw[:, VECTOR_COLS:], math.sqrt(C))
+            start = 0
+            for width in load_widths(b):
+                cut = start + 2 * width // 3 // 8 * 8
+                end = start + width
+                nc.sync.dma_start(xs_b[:, start:end], emb[channels, start:end])
+                nc.vector.tensor_scalar_mul(xs_b[:, start:cut], xs_b[:, start:cut], math.sqrt(C))
+                nc.scalar.mul(xs_b[:, cut:end], xs_b[:, cut:end], math.sqrt(C))
+                start = end
 
             first, last = b == 0, b == BLOCKS - 1
             for t in range(PIECES):
@@ -109,7 +118,7 @@ def tile_blockdiffusiondecoder_kernel(tc, emb, pos, ln_emb_s, ln_emb_b, offs, ou
                     out_piece[:],
                     normed[:],
                     ACT.Identity,
-                    bias=bias[:, b : b + 1],
-                    scale=gain[:, b : b + 1],
+                    bias=gain_bias[:, BLOCKS + b : BLOCKS + b + 1],
+                    scale=gain_bias[:, b : b + 1],
                 )
                 nc.sync.dma_start(out[b * P : (b + 1) * P, t * M : (t + 1) * M], out_piece[:])

@@ -46,6 +46,8 @@ def tile_blockdiffusiondecoder_kernel(tc, emb, pos, ln_emb_s, ln_emb_b, offs, ou
         nc.gpsimd.memset(block_mean_w[:], 1.0 / P)
         mean_w = held.tile([P, P], F32, name="mean_w")
         nc.gpsimd.memset(mean_w[:], 1.0 / C)
+        minus_row_mean_w = held.tile([P, P], F32, name="minus_row_mean_w")
+        nc.gpsimd.memset(minus_row_mean_w[:], -1.0 / P)
         eps = held.tile([P, 1], F32, name="eps")
         nc.gpsimd.memset(eps[:], EPS)
 
@@ -54,9 +56,9 @@ def tile_blockdiffusiondecoder_kernel(tc, emb, pos, ln_emb_s, ln_emb_b, offs, ou
 
         pivot_ps = [psum.tile([P, M], F32, name=f"pivot_ps{t}") for t in range(PIECES)]
         m_ps = [psum.tile([P, M], F32, name=f"m_ps{t}") for t in range(PIECES)]
-        q_ps = [psum.tile([P, M], F32, name=f"q_ps{t}") for t in range(PIECES)]
+        var_ps = [psum.tile([P, M], F32, name=f"var_ps{t}") for t in range(PIECES)]
 
-        d = {}
+        d = [held.tile([P, BLOCKS, M], F32, name=f"d{t}") for t in range(PIECES)]
         for b in range(BLOCKS):
             channels = slice(b * P, (b + 1) * P)
             pos_b = held.tile([P, N], F32, name=f"pos{b}")
@@ -76,43 +78,38 @@ def tile_blockdiffusiondecoder_kernel(tc, emb, pos, ln_emb_s, ln_emb_b, offs, ou
             for t in range(PIECES):
                 looked_up = xs_b[:].indirect(offsets[:, t * (M // 16) : (t + 1) * (M // 16)])
                 pos_piece = pos_b[:, t * M : (t + 1) * M]
-                d[b, t] = held.tile([P, M], F32, name=f"d{b}_{t}")
+                d_block = d[t][:, b, :]
                 if first:
                     h0 = held.tile([P, M], F32, name=f"h0_{t}")
                     nc.vector.tensor_tensor(h0[:], looked_up, pos_piece, ALU.add)
                     nc.tensor.matmul(pivot_ps[t][:], block_mean_w[:], h0[:], start=True, stop=True)
-                    nc.vector.tensor_tensor(d[b, t][:], h0[:], pivot_ps[t][:], ALU.subtract)
+                    nc.vector.tensor_tensor(d_block, h0[:], pivot_ps[t][:], ALU.subtract)
                 else:
                     shifted = held.tile([P, M], F32, name=f"shifted{b}_{t}")
                     nc.vector.tensor_tensor(shifted[:], pos_piece, pivot_ps[t][:], ALU.subtract)
-                    nc.vector.tensor_tensor(d[b, t][:], looked_up, shifted[:], ALU.add)
+                    nc.vector.tensor_tensor(d_block, looked_up, shifted[:], ALU.add)
                 sq = held.tile([P, M], F32, name=f"sq{b}_{t}")
-                nc.scalar.square(sq[:], d[b, t][:])
-                nc.tensor.matmul(m_ps[t][:], mean_w[:], d[b, t][:], start=first, stop=last)
-                nc.tensor.matmul(q_ps[t][:], mean_w[:], sq[:], start=first, stop=last)
+                nc.scalar.square(sq[:], d_block)
+                nc.tensor.matmul(m_ps[t][:], mean_w[:], d_block, start=first, stop=last)
+                nc.tensor.matmul(var_ps[t][:], mean_w[:], sq[:], start=first, stop=False)
 
-        m, rstd = [], []
+        centred, rstd = [], []
         for t in range(PIECES):
-            m_t = held.tile([P, M], F32, name=f"m{t}")
-            nc.scalar.copy(m_t[:], m_ps[t][:])
             m_squared = held.tile([P, M], F32, name=f"m_squared{t}")
             nc.scalar.square(m_squared[:], m_ps[t][:])
-            var = held.tile([P, M], F32, name=f"var{t}")
-            nc.vector.tensor_tensor(var[:], q_ps[t][:], m_squared[:], ALU.subtract)
+            nc.tensor.matmul(var_ps[t][:], minus_row_mean_w[:], m_squared[:], start=False, stop=True)
+            centred_t = held.tile([P, BLOCKS, M], F32, name=f"centred{t}")
+            m_for_each_block = m_ps[t][:].unsqueeze(1).to_broadcast([P, BLOCKS, M])
+            nc.vector.tensor_tensor(centred_t[:], d[t][:], m_for_each_block, ALU.subtract)
+            centred.append(centred_t)
             rstd_t = held.tile([P, M], F32, name=f"rstd{t}")
-            nc.scalar.activation(rstd_t[:], var[:], ACT.Abs_reciprocal_sqrt, bias=eps[:])
-            m.append(m_t)
+            nc.scalar.activation(rstd_t[:], var_ps[t][:], ACT.Abs_reciprocal_sqrt, bias=eps[:])
             rstd.append(rstd_t)
 
         for t in range(PIECES):
-            centred = []
-            for b in range(BLOCKS):
-                centred_b = held.tile([P, M], F32, name=f"centred{b}_{t}")
-                nc.vector.tensor_tensor(centred_b[:], d[b, t][:], m[t][:], ALU.subtract)
-                centred.append(centred_b)
             for b in range(BLOCKS):
                 normed = held.tile([P, M], F32, name=f"normed{b}_{t}")
-                nc.vector.tensor_tensor(normed[:], centred[b][:], rstd[t][:], ALU.mult)
+                nc.vector.tensor_tensor(normed[:], centred[t][:, b, :], rstd[t][:], ALU.mult)
                 out_piece = held.tile([P, M], F32, name=f"out{b}_{t}")
                 nc.scalar.activation(
                     out_piece[:],

@@ -59,6 +59,7 @@ def tile_blockdiffusiondecoder_kernel(tc, emb, pos, ln_emb_s, ln_emb_b, offs, ou
         var_ps = [psum.tile([P, M], F32, name=f"var_ps{t}") for t in range(PIECES)]
 
         d = [held.tile([P, BLOCKS, M], F32, name=f"d{t}") for t in range(PIECES)]
+        centred, rstd = [], []
         for b in range(BLOCKS):
             channels = slice(b * P, (b + 1) * P)
             pos_b = held.tile([P, N], F32, name=f"pos{b}")
@@ -88,23 +89,25 @@ def tile_blockdiffusiondecoder_kernel(tc, emb, pos, ln_emb_s, ln_emb_b, offs, ou
                     shifted = held.tile([P, M], F32, name=f"shifted{b}_{t}")
                     nc.vector.tensor_tensor(shifted[:], pos_piece, pivot_ps[t][:], ALU.subtract)
                     nc.vector.tensor_tensor(d_block, looked_up, shifted[:], ALU.add)
-                sq = held.tile([P, M], F32, name=f"sq{b}_{t}")
-                nc.scalar.square(sq[:], d_block)
                 nc.tensor.matmul(m_ps[t][:], mean_w[:], d_block, start=first, stop=last)
-                nc.tensor.matmul(var_ps[t][:], mean_w[:], sq[:], start=first, stop=False)
 
-        centred, rstd = [], []
-        for t in range(PIECES):
-            m_squared = held.tile([P, M], F32, name=f"m_squared{t}")
-            nc.scalar.square(m_squared[:], m_ps[t][:])
-            nc.tensor.matmul(var_ps[t][:], minus_row_mean_w[:], m_squared[:], start=False, stop=True)
-            centred_t = held.tile([P, BLOCKS, M], F32, name=f"centred{t}")
-            m_for_each_block = m_ps[t][:].unsqueeze(1).to_broadcast([P, BLOCKS, M])
-            nc.vector.tensor_tensor(centred_t[:], d[t][:], m_for_each_block, ALU.subtract)
-            centred.append(centred_t)
-            rstd_t = held.tile([P, M], F32, name=f"rstd{t}")
-            nc.scalar.activation(rstd_t[:], var_ps[t][:], ACT.Abs_reciprocal_sqrt, bias=eps[:])
-            rstd.append(rstd_t)
+            for t in range(PIECES):
+                sq = held.tile([P, M], F32, name=f"sq{b}_{t}")
+                nc.scalar.square(sq[:], d[t][:, b, :])
+                nc.tensor.matmul(var_ps[t][:], mean_w[:], sq[:], start=first, stop=False)
+                if not last:
+                    continue
+
+                m_squared = held.tile([P, M], F32, name=f"m_squared{t}")
+                nc.scalar.square(m_squared[:], m_ps[t][:])
+                nc.tensor.matmul(var_ps[t][:], minus_row_mean_w[:], m_squared[:], start=False, stop=True)
+                centred_t = held.tile([P, BLOCKS, M], F32, name=f"centred{t}")
+                m_for_each_block = m_ps[t][:].unsqueeze(1).to_broadcast([P, BLOCKS, M])
+                nc.vector.tensor_tensor(centred_t[:], d[t][:], m_for_each_block, ALU.subtract)
+                centred.append(centred_t)
+                rstd_t = held.tile([P, M], F32, name=f"rstd{t}")
+                nc.scalar.activation(rstd_t[:], var_ps[t][:], ACT.Abs_reciprocal_sqrt, bias=eps[:])
+                rstd.append(rstd_t)
 
         for t in range(PIECES):
             for b in range(BLOCKS):

@@ -6,8 +6,12 @@ from concourse.masks import make_identity
 P = 128
 C, S, N = 512, 4096, 512
 BLOCKS = C // P
-PIECES = 2
-M = N // PIECES
+TILES = N // P
+HALVES = 2
+PER_HALF = TILES // HALVES
+M = N // HALVES
+PAIRS = BLOCKS // 2
+STATS = 6
 EPS = 1e-5
 FLOPS = C * S + 8 * C * N
 
@@ -27,7 +31,7 @@ def tile_blockdiffusiondecoder_kernel(tc, emb, pos, ln_emb_s, ln_emb_b, offs, ou
     nc = tc.nc
     with (
         tc.tile_pool(name="held", bufs=1) as held,
-        tc.psum_pool(name="psum", bufs=1) as psum,
+        tc.psum_pool(name="psum", bufs=8) as psum,
     ):
         offsets = held.tile([P, N // 16], U16, name="offsets")
         nc.sync.dma_start(offsets[:], offs)
@@ -35,33 +39,29 @@ def tile_blockdiffusiondecoder_kernel(tc, emb, pos, ln_emb_s, ln_emb_b, offs, ou
         rows = held.tile([2 * BLOCKS, P], F32, name="rows")
         nc.scalar.dma_start(rows[:BLOCKS, :], ln_emb_s.rearrange("(b p) o -> b (p o)", p=P))
         nc.scalar.dma_start(rows[BLOCKS:, :], ln_emb_b.rearrange("(b p) o -> b (p o)", p=P))
-        identity = held.tile([2 * BLOCKS, 2 * BLOCKS], F32, name="identity")
+        identity = held.tile([P, P], F32, name="identity")
         make_identity(nc, identity[:])
-        gain_bias_ps = psum.tile([P, 2 * BLOCKS], F32, name="gain_bias_ps")
-        nc.tensor.matmul(gain_bias_ps[:], rows[:], identity[:], start=True, stop=True)
+        gain_bias_ps = psum.tile([P, N], F32, name="gain_bias_ps", tag="bank")
+        nc.tensor.matmul(
+            gain_bias_ps[:, : 2 * BLOCKS], rows[:], identity[: 2 * BLOCKS, : 2 * BLOCKS], start=True, stop=True
+        )
         gain_bias = held.tile([P, 2 * BLOCKS], F32, name="gain_bias")
-        nc.vector.tensor_copy(gain_bias[:], gain_bias_ps[:])
+        nc.vector.tensor_copy(gain_bias[:], gain_bias_ps[:, : 2 * BLOCKS])
 
-        block_mean_w = held.tile([P, P], F32, name="block_mean_w")
-        nc.gpsimd.memset(block_mean_w[:], 1.0 / P)
-        mean_w = held.tile([P, P], F32, name="mean_w")
-        nc.gpsimd.memset(mean_w[:], 1.0 / C)
-        minus_row_mean_w = held.tile([P, P], F32, name="minus_row_mean_w")
-        nc.gpsimd.memset(minus_row_mean_w[:], -1.0 / P)
         eps = held.tile([P, 1], F32, name="eps")
         nc.gpsimd.memset(eps[:], EPS)
 
         warm = held.tile([P, 1], F32, name="warm")
         nc.scalar.activation(warm[:], eps[:], ACT.Abs_reciprocal_sqrt)
 
-        pivot_ps = [psum.tile([P, M], F32, name=f"pivot_ps{t}") for t in range(PIECES)]
-        m_ps = [psum.tile([P, M], F32, name=f"m_ps{t}") for t in range(PIECES)]
-        var_ps = [psum.tile([P, M], F32, name=f"var_ps{t}") for t in range(PIECES)]
+        h_tokens = held.tile([P, TILES, C], F32, name="h_tokens")
+        normed = held.tile([P, TILES, C], F32, name="normed")
+        stats = held.tile([P, TILES, PAIRS * STATS], F32, name="stats")
+        mean_var = held.tile([P, TILES, 2], F32, name="mean_var")
 
-        d = [held.tile([P, BLOCKS, M], F32, name=f"d{t}") for t in range(PIECES)]
-        centred, rstd = [], []
         for b in range(BLOCKS):
             channels = slice(b * P, (b + 1) * P)
+            pair, first, last = b // 2, b % 2 == 0, b == BLOCKS - 1
             pos_b = held.tile([P, N], F32, name=f"pos{b}")
             nc.sync.dma_start(pos_b[:], pos[channels, :])
 
@@ -75,50 +75,58 @@ def tile_blockdiffusiondecoder_kernel(tc, emb, pos, ln_emb_s, ln_emb_b, offs, ou
                 nc.scalar.mul(xs_b[:, cut:end], xs_b[:, cut:end], math.sqrt(C))
                 start = end
 
-            first, last = b == 0, b == BLOCKS - 1
-            for t in range(PIECES):
-                looked_up = xs_b[:].indirect(offsets[:, t * (M // 16) : (t + 1) * (M // 16)])
-                pos_piece = pos_b[:, t * M : (t + 1) * M]
-                d_block = d[t][:, b, :]
-                if first:
-                    h0 = held.tile([P, M], F32, name=f"h0_{t}")
-                    nc.vector.tensor_tensor(h0[:], looked_up, pos_piece, ALU.add)
-                    nc.tensor.matmul(pivot_ps[t][:], block_mean_w[:], h0[:], start=True, stop=True)
-                    nc.vector.tensor_tensor(d_block, h0[:], pivot_ps[t][:], ALU.subtract)
-                else:
-                    shifted = held.tile([P, M], F32, name=f"shifted{b}_{t}")
-                    nc.vector.tensor_tensor(shifted[:], pos_piece, pivot_ps[t][:], ALU.subtract)
-                    nc.vector.tensor_tensor(d_block, looked_up, shifted[:], ALU.add)
-                nc.tensor.matmul(m_ps[t][:], mean_w[:], d_block, start=first, stop=last)
+            h_b = held.tile([P, N], F32, name=f"h{b}")
+            if last:
+                for t in range(HALVES):
+                    half = slice(t * M, (t + 1) * M)
+                    looked_up = xs_b[:].indirect(offsets[:, t * (M // 16) : (t + 1) * (M // 16)])
+                    nc.vector.tensor_tensor(h_b[:, half], looked_up, pos_b[:, half], ALU.add)
+            else:
+                nc.vector.tensor_tensor(h_b[:], xs_b[:].indirect(offsets[:]), pos_b[:], ALU.add)
 
-            for t in range(PIECES):
-                sq = held.tile([P, M], F32, name=f"sq{b}_{t}")
-                nc.scalar.square(sq[:], d[t][:, b, :])
-                nc.tensor.matmul(var_ps[t][:], mean_w[:], sq[:], start=first, stop=False)
-                if not last:
-                    continue
+            if first:
+                turned = [psum.tile([P, 2 * P], F32, name=f"turned{pair}_{i}", tag="bank") for i in range(TILES)]
+            for i in range(TILES):
+                side = turned[i][:, :P] if first else turned[i][:, P:]
+                nc.tensor.transpose(side, h_b[:, i * P : (i + 1) * P], identity[:])
+            if first:
+                continue
+            for t in range(HALVES):
+                tiles = range(t * PER_HALF, (t + 1) * PER_HALF)
+                for i in tiles:
+                    nc.vector.bn_stats(stats[:, i, pair * STATS : (pair + 1) * STATS], turned[i][:])
+                if last:
+                    for i in tiles:
+                        nc.vector.bn_aggr(mean_var[:, i, :], stats[:, i, :])
+                for i in tiles:
+                    nc.scalar.copy(h_tokens[:, i, pair * 2 * P : (pair + 1) * 2 * P], turned[i][:])
 
-                m_squared = held.tile([P, M], F32, name=f"m_squared{t}")
-                nc.scalar.square(m_squared[:], m_ps[t][:])
-                nc.tensor.matmul(var_ps[t][:], minus_row_mean_w[:], m_squared[:], start=False, stop=True)
-                centred_t = held.tile([P, BLOCKS, M], F32, name=f"centred{t}")
-                m_for_each_block = m_ps[t][:].unsqueeze(1).to_broadcast([P, BLOCKS, M])
-                nc.vector.tensor_tensor(centred_t[:], d[t][:], m_for_each_block, ALU.subtract)
-                centred.append(centred_t)
-                rstd_t = held.tile([P, M], F32, name=f"rstd{t}")
-                nc.scalar.activation(rstd_t[:], var_ps[t][:], ACT.Abs_reciprocal_sqrt, bias=eps[:])
-                rstd.append(rstd_t)
+        rstd = []
+        for t in range(HALVES):
+            rstd_t = held.tile([P, PER_HALF], F32, name=f"rstd{t}")
+            variances = mean_var[:, t * PER_HALF : (t + 1) * PER_HALF, 1]
+            nc.scalar.activation(rstd_t[:], variances, ACT.Abs_reciprocal_sqrt, bias=eps[:])
+            rstd.append(rstd_t)
 
-        for t in range(PIECES):
-            for b in range(BLOCKS):
-                normed = held.tile([P, M], F32, name=f"normed{b}_{t}")
-                nc.vector.tensor_tensor(normed[:], centred[t][:, b, :], rstd[t][:], ALU.mult)
-                out_piece = held.tile([P, M], F32, name=f"out{b}_{t}")
-                nc.scalar.activation(
-                    out_piece[:],
-                    normed[:],
-                    ACT.Identity,
-                    bias=gain_bias[:, BLOCKS + b : BLOCKS + b + 1],
-                    scale=gain_bias[:, b : b + 1],
+        for t in range(HALVES):
+            back = [psum.tile([P, N], F32, name=f"back{t}_{b}", tag="bank") for b in range(BLOCKS)]
+            for k in range(PER_HALF):
+                i = t * PER_HALF + k
+                nc.vector.tensor_scalar(
+                    normed[:, i, :],
+                    h_tokens[:, i, :],
+                    mean_var[:, i, 0:1],
+                    rstd[t][:, k : k + 1],
+                    ALU.subtract,
+                    ALU.mult,
                 )
+                for b in range(BLOCKS):
+                    nc.tensor.transpose(back[b][:, k * P : (k + 1) * P], normed[:, i, b * P : (b + 1) * P], identity[:])
+            for b in range(BLOCKS):
+                out_piece = held.tile([P, M], F32, name=f"out{t}_{b}")
+                gain, bias = gain_bias[:, b : b + 1], gain_bias[:, BLOCKS + b : BLOCKS + b + 1]
+                if t == HALVES - 1 and b % 2 == 1:
+                    nc.vector.tensor_scalar(out_piece[:], back[b][:, :M], gain, bias, ALU.mult, ALU.add)
+                else:
+                    nc.scalar.activation(out_piece[:], back[b][:, :M], ACT.Identity, bias=bias, scale=gain)
                 nc.sync.dma_start(out[b * P : (b + 1) * P, t * M : (t + 1) * M], out_piece[:])

@@ -24,7 +24,7 @@ ACT = mybir.ActivationFunctionType
 def load_widths(b):
     if b < BLOCKS - 1:
         return [S]
-    return [S // 2, S // 4, S // 8, S // 8]
+    return [S // 2, S // 4, S // 8, S // 16, S // 16]
 
 
 def tile_blockdiffusiondecoder_kernel(tc, emb, pos, ln_emb_s, ln_emb_b, offs, out):
@@ -59,6 +59,10 @@ def tile_blockdiffusiondecoder_kernel(tc, emb, pos, ln_emb_s, ln_emb_b, offs, ou
         stats = held.tile([P, TILES, PAIRS * STATS], F32, name="stats")
         mean_var = held.tile([P, TILES, 2], F32, name="mean_var")
 
+        def keep(pair, turned, i):
+            nc.vector.bn_stats(stats[:, i, pair * STATS : (pair + 1) * STATS], turned[i][:])
+            nc.scalar.copy(h_tokens[:, i, pair * 2 * P : (pair + 1) * 2 * P], turned[i][:])
+
         for b in range(BLOCKS):
             channels = slice(b * P, (b + 1) * P)
             pair, first, last = b // 2, b % 2 == 0, b == BLOCKS - 1
@@ -89,26 +93,20 @@ def tile_blockdiffusiondecoder_kernel(tc, emb, pos, ln_emb_s, ln_emb_b, offs, ou
             for i in range(TILES):
                 side = turned[i][:, :P] if first else turned[i][:, P:]
                 nc.tensor.transpose(side, h_b[:, i * P : (i + 1) * P], identity[:])
-            if first:
-                continue
-            for t in range(HALVES):
-                tiles = range(t * PER_HALF, (t + 1) * PER_HALF)
-                for i in tiles:
-                    nc.vector.bn_stats(stats[:, i, pair * STATS : (pair + 1) * STATS], turned[i][:])
-                if last:
-                    for i in tiles:
-                        nc.vector.bn_aggr(mean_var[:, i, :], stats[:, i, :])
-                for i in tiles:
-                    nc.scalar.copy(h_tokens[:, i, pair * 2 * P : (pair + 1) * 2 * P], turned[i][:])
+            if not first and not last:
+                for i in range(TILES):
+                    keep(pair, turned, i)
 
         rstd = []
         for t in range(HALVES):
-            rstd_t = held.tile([P, PER_HALF], F32, name=f"rstd{t}")
-            variances = mean_var[:, t * PER_HALF : (t + 1) * PER_HALF, 1]
-            nc.scalar.activation(rstd_t[:], variances, ACT.Abs_reciprocal_sqrt, bias=eps[:])
-            rstd.append(rstd_t)
+            tiles = range(t * PER_HALF, (t + 1) * PER_HALF)
+            for i in tiles:
+                keep(pair, turned, i)
+                nc.vector.bn_aggr(mean_var[:, i, :], stats[:, i, :])
+                rstd_i = held.tile([P, 1], F32, name=f"rstd{i}")
+                nc.scalar.activation(rstd_i[:], mean_var[:, i, 1:2], ACT.Abs_reciprocal_sqrt, bias=eps[:])
+                rstd.append(rstd_i)
 
-        for t in range(HALVES):
             back = [psum.tile([P, N], F32, name=f"back{t}_{b}", tag="bank") for b in range(BLOCKS)]
             for k in range(PER_HALF):
                 i = t * PER_HALF + k
@@ -116,7 +114,7 @@ def tile_blockdiffusiondecoder_kernel(tc, emb, pos, ln_emb_s, ln_emb_b, offs, ou
                     normed[:, i, :],
                     h_tokens[:, i, :],
                     mean_var[:, i, 0:1],
-                    rstd[t][:, k : k + 1],
+                    rstd[i][:],
                     ALU.subtract,
                     ALU.mult,
                 )
@@ -125,7 +123,7 @@ def tile_blockdiffusiondecoder_kernel(tc, emb, pos, ln_emb_s, ln_emb_b, offs, ou
             for b in range(BLOCKS):
                 out_piece = held.tile([P, M], F32, name=f"out{t}_{b}")
                 gain, bias = gain_bias[:, b : b + 1], gain_bias[:, BLOCKS + b : BLOCKS + b + 1]
-                if t == HALVES - 1 and b % 2 == 1:
+                if b % 2 == 1:
                     nc.vector.tensor_scalar(out_piece[:], back[b][:, :M], gain, bias, ALU.mult, ALU.add)
                 else:
                     nc.scalar.activation(out_piece[:], back[b][:, :M], ACT.Identity, bias=bias, scale=gain)

@@ -66,15 +66,15 @@ def tile_blockdiffusiondecoder_kernel(tc, emb, pos, ln_emb_s, ln_emb_b, offs, ou
         for b in range(BLOCKS):
             channels = slice(b * P, (b + 1) * P)
             pair, first, last = b // 2, b % 2 == 0, b == BLOCKS - 1
-            pos_b = held.tile([P, N], F32, name=f"pos{b}")
-            nc.sync.dma_start(pos_b[:], pos[channels, :])
-
             xs_b = held.tile([P, S], F32, name=f"xs{b}")
             start = 0
             for width in load_widths(b):
                 cut = start + 2 * width // 3 // 8 * 8
                 end = start + width
                 nc.sync.dma_start(xs_b[:, start:end], emb[channels, start:end])
+                if start == 0:
+                    pos_b = held.tile([P, N], F32, name=f"pos{b}")
+                    nc.sync.dma_start(pos_b[:], pos[channels, :])
                 nc.vector.tensor_scalar_mul(xs_b[:, start:cut], xs_b[:, start:cut], math.sqrt(C))
                 nc.scalar.mul(xs_b[:, cut:end], xs_b[:, cut:end], math.sqrt(C))
                 start = end

@@ -54,14 +54,10 @@ def tile_blockdiffusiondecoder_kernel(tc, emb, pos, ln_emb_s, ln_emb_b, offs, ou
         warm = held.tile([P, 1], F32, name="warm")
         nc.scalar.activation(warm[:], eps[:], ACT.Abs_reciprocal_sqrt)
 
-        h_tokens = held.tile([P, TILES, C], F32, name="h_tokens")
+        h_first = held.tile([P, TILES, 2 * P], F32, name="h_first")
         normed = held.tile([P, TILES, C], F32, name="normed")
         stats = held.tile([P, TILES, PAIRS * STATS], F32, name="stats")
         mean_var = held.tile([P, TILES, 2], F32, name="mean_var")
-
-        def keep(pair, turned, i):
-            nc.vector.bn_stats(stats[:, i, pair * STATS : (pair + 1) * STATS], turned[i][:])
-            nc.scalar.copy(h_tokens[:, i, pair * 2 * P : (pair + 1) * 2 * P], turned[i][:])
 
         for b in range(BLOCKS):
             channels = slice(b * P, (b + 1) * P)
@@ -95,28 +91,32 @@ def tile_blockdiffusiondecoder_kernel(tc, emb, pos, ln_emb_s, ln_emb_b, offs, ou
                 nc.tensor.transpose(side, h_b[:, i * P : (i + 1) * P], identity[:])
             if not first and not last:
                 for i in range(TILES):
-                    keep(pair, turned, i)
+                    nc.vector.bn_stats(stats[:, i, :STATS], turned[i][:])
+                    nc.scalar.copy(h_first[:, i, :], turned[i][:])
 
-        rstd = []
+        rstd, shift = [], []
         for t in range(HALVES):
             tiles = range(t * PER_HALF, (t + 1) * PER_HALF)
             for i in tiles:
-                keep(pair, turned, i)
+                nc.vector.bn_stats(stats[:, i, STATS:], turned[i][:])
                 nc.vector.bn_aggr(mean_var[:, i, :], stats[:, i, :])
                 rstd_i = held.tile([P, 1], F32, name=f"rstd{i}")
                 nc.scalar.activation(rstd_i[:], mean_var[:, i, 1:2], ACT.Abs_reciprocal_sqrt, bias=eps[:])
                 rstd.append(rstd_i)
+                shift_i = held.tile([P, 1], F32, name=f"shift{i}")
+                nc.vector.scalar_tensor_tensor(
+                    shift_i[:], mean_var[:, i, 0:1], -1.0, rstd_i[:], ALU.mult, ALU.mult
+                )
+                shift.append(shift_i)
 
             back = [psum.tile([P, N], F32, name=f"back{t}_{b}", tag="bank") for b in range(BLOCKS)]
             for k in range(PER_HALF):
                 i = t * PER_HALF + k
                 nc.vector.tensor_scalar(
-                    normed[:, i, :],
-                    h_tokens[:, i, :],
-                    mean_var[:, i, 0:1],
-                    rstd[i][:],
-                    ALU.subtract,
-                    ALU.mult,
+                    normed[:, i, : 2 * P], h_first[:, i, :], mean_var[:, i, 0:1], rstd[i][:], ALU.subtract, ALU.mult
+                )
+                nc.scalar.activation(
+                    normed[:, i, 2 * P :], turned[i][:], ACT.Identity, bias=shift[i][:], scale=rstd[i][:]
                 )
                 for b in range(BLOCKS):
                     nc.tensor.transpose(back[b][:, k * P : (k + 1) * P], normed[:, i, b * P : (b + 1) * P], identity[:])

@@ -123,7 +123,7 @@ def tile_blockdiffusiondecoder_kernel(tc, emb, pos, ln_emb_s, ln_emb_b, offs, ou
             for b in range(BLOCKS):
                 out_piece = held.tile([P, M], F32, name=f"out{t}_{b}")
                 gain, bias = gain_bias[:, b : b + 1], gain_bias[:, BLOCKS + b : BLOCKS + b + 1]
-                if b % 2 == 1:
+                if t == HALVES - 1 and b % 2 == 1:
                     nc.vector.tensor_scalar(out_piece[:], back[b][:, :M], gain, bias, ALU.mult, ALU.add)
                 else:
                     nc.scalar.activation(out_piece[:], back[b][:, :M], ACT.Identity, bias=bias, scale=gain)

@@ -94,7 +94,7 @@ def tile_blockdiffusiondecoder_kernel(tc, emb, pos, ln_emb_s, ln_emb_b, offs, ou
                     nc.vector.bn_stats(stats[:, i, :STATS], turned[i][:])
                     nc.scalar.copy(h_first[:, i, :], turned[i][:])
 
-        rstd, shift = [], []
+        rstd = []
         for t in range(HALVES):
             tiles = range(t * PER_HALF, (t + 1) * PER_HALF)
             for i in tiles:
@@ -103,21 +103,24 @@ def tile_blockdiffusiondecoder_kernel(tc, emb, pos, ln_emb_s, ln_emb_b, offs, ou
                 rstd_i = held.tile([P, 1], F32, name=f"rstd{i}")
                 nc.scalar.activation(rstd_i[:], mean_var[:, i, 1:2], ACT.Abs_reciprocal_sqrt, bias=eps[:])
                 rstd.append(rstd_i)
-                shift_i = held.tile([P, 1], F32, name=f"shift{i}")
-                nc.vector.scalar_tensor_tensor(
-                    shift_i[:], mean_var[:, i, 0:1], -1.0, rstd_i[:], ALU.mult, ALU.mult
-                )
-                shift.append(shift_i)
 
             back = [psum.tile([P, N], F32, name=f"back{t}_{b}", tag="bank") for b in range(BLOCKS)]
             for k in range(PER_HALF):
                 i = t * PER_HALF + k
+                mean, one_rstd = mean_var[:, i, 0:1], rstd[i][:]
                 nc.vector.tensor_scalar(
-                    normed[:, i, : 2 * P], h_first[:, i, :], mean_var[:, i, 0:1], rstd[i][:], ALU.subtract, ALU.mult
+                    normed[:, i, : 2 * P], h_first[:, i, :], mean, one_rstd, ALU.subtract, ALU.mult
                 )
-                nc.scalar.activation(
-                    normed[:, i, 2 * P :], turned[i][:], ACT.Identity, bias=shift[i][:], scale=rstd[i][:]
-                )
+                if t == HALVES - 1:
+                    nc.vector.tensor_scalar(
+                        normed[:, i, 2 * P :], turned[i][:], mean, one_rstd, ALU.subtract, ALU.mult
+                    )
+                else:
+                    shift = held.tile([P, 1], F32, name=f"shift{i}")
+                    nc.vector.scalar_tensor_tensor(shift[:], mean, -1.0, one_rstd, ALU.mult, ALU.mult)
+                    nc.scalar.activation(
+                        normed[:, i, 2 * P :], turned[i][:], ACT.Identity, bias=shift[:], scale=one_rstd
+                    )
                 for b in range(BLOCKS):
                     nc.tensor.transpose(back[b][:, k * P : (k + 1) * P], normed[:, i, b * P : (b + 1) * P], identity[:])
             for b in range(BLOCKS):

import math

import concourse.mybir as mybir
from concourse.masks import make_identity

P = 128
C, S, N = 512, 4096, 512
BLOCKS = C // P
TILES = N // P
HALVES = 2
PER_HALF = TILES // HALVES
M = N // HALVES
PAIRS = BLOCKS // 2
STATS = 6
EPS = 1e-5
FLOPS = C * S + 8 * C * N

F32 = mybir.dt.float32
U16 = mybir.dt.uint16
ALU = mybir.AluOpType
ACT = mybir.ActivationFunctionType


def load_widths(b):
    if b < BLOCKS - 1:
        return [S]
    return [S // 2, S // 4, S // 8, S // 16, S // 16]


def tile_blockdiffusiondecoder_kernel(tc, emb, pos, ln_emb_s, ln_emb_b, offs, out):
    nc = tc.nc
    with (
        tc.tile_pool(name="held", bufs=1) as held,
        tc.psum_pool(name="psum", bufs=8) as psum,
    ):
        offsets = held.tile([P, N // 16], U16, name="offsets")
        nc.sync.dma_start(offsets[:], offs)

        rows = held.tile([2 * BLOCKS, P], F32, name="rows")
        nc.scalar.dma_start(rows[:BLOCKS, :], ln_emb_s.rearrange("(b p) o -> b (p o)", p=P))
        nc.scalar.dma_start(rows[BLOCKS:, :], ln_emb_b.rearrange("(b p) o -> b (p o)", p=P))
        identity = held.tile([P, P], F32, name="identity")
        make_identity(nc, identity[:])
        gain_bias_ps = psum.tile([P, N], F32, name="gain_bias_ps", tag="bank")
        nc.tensor.matmul(
            gain_bias_ps[:, : 2 * BLOCKS], rows[:], identity[: 2 * BLOCKS, : 2 * BLOCKS], start=True, stop=True
        )
        gain_bias = held.tile([P, 2 * BLOCKS], F32, name="gain_bias")
        nc.vector.tensor_copy(gain_bias[:], gain_bias_ps[:, : 2 * BLOCKS])

        eps = held.tile([P, 1], F32, name="eps")
        nc.gpsimd.memset(eps[:], EPS)

        warm = held.tile([P, 1], F32, name="warm")
        nc.scalar.activation(warm[:], eps[:], ACT.Abs_reciprocal_sqrt)

        h_first = held.tile([P, TILES, 2 * P], F32, name="h_first")
        normed = held.tile([P, TILES, C], F32, name="normed")
        stats = held.tile([P, TILES, PAIRS * STATS], F32, name="stats")
        mean_var = held.tile([P, TILES, 2], F32, name="mean_var")

        for b in range(BLOCKS):
            channels = slice(b * P, (b + 1) * P)
            pair, first, last = b // 2, b % 2 == 0, b == BLOCKS - 1
            xs_b = held.tile([P, S], F32, name=f"xs{b}")
            start = 0
            for width in load_widths(b):
                cut = start + 2 * width // 3 // 8 * 8
                end = start + width
                nc.sync.dma_start(xs_b[:, start:end], emb[channels, start:end])
                if start == 0:
                    pos_b = held.tile([P, N], F32, name=f"pos{b}")
                    nc.sync.dma_start(pos_b[:], pos[channels, :])
                nc.vector.tensor_scalar_mul(xs_b[:, start:cut], xs_b[:, start:cut], math.sqrt(C))
                nc.scalar.mul(xs_b[:, cut:end], xs_b[:, cut:end], math.sqrt(C))
                start = end

            h_b = held.tile([P, N], F32, name=f"h{b}")
            if last:
                for t in range(HALVES):
                    half = slice(t * M, (t + 1) * M)
                    looked_up = xs_b[:].indirect(offsets[:, t * (M // 16) : (t + 1) * (M // 16)])
                    nc.vector.tensor_tensor(h_b[:, half], looked_up, pos_b[:, half], ALU.add)
            else:
                nc.vector.tensor_tensor(h_b[:], xs_b[:].indirect(offsets[:]), pos_b[:], ALU.add)

            if first:
                turned = [psum.tile([P, 2 * P], F32, name=f"turned{pair}_{i}", tag="bank") for i in range(TILES)]
            for i in range(TILES):
                side = turned[i][:, :P] if first else turned[i][:, P:]
                nc.tensor.transpose(side, h_b[:, i * P : (i + 1) * P], identity[:])
            if not first and not last:
                for i in range(TILES):
                    nc.vector.bn_stats(stats[:, i, :STATS], turned[i][:])
                    nc.scalar.copy(h_first[:, i, :], turned[i][:])

        rstd = []
        for t in range(HALVES):
            tiles = range(t * PER_HALF, (t + 1) * PER_HALF)
            for i in tiles:
                nc.vector.bn_stats(stats[:, i, STATS:], turned[i][:])
                nc.vector.bn_aggr(mean_var[:, i, :], stats[:, i, :])
                rstd_i = held.tile([P, 1], F32, name=f"rstd{i}")
                nc.scalar.activation(rstd_i[:], mean_var[:, i, 1:2], ACT.Abs_reciprocal_sqrt, bias=eps[:])
                rstd.append(rstd_i)

            back = [psum.tile([P, N], F32, name=f"back{t}_{b}", tag="bank") for b in range(BLOCKS)]
            for k in range(PER_HALF):
                i = t * PER_HALF + k
                mean, one_rstd = mean_var[:, i, 0:1], rstd[i][:]
                nc.vector.tensor_scalar(
                    normed[:, i, : 2 * P], h_first[:, i, :], mean, one_rstd, ALU.subtract, ALU.mult
                )
                if t == HALVES - 1:
                    nc.vector.tensor_scalar(
                        normed[:, i, 2 * P :], turned[i][:], mean, one_rstd, ALU.subtract, ALU.mult
                    )
                else:
                    shift = held.tile([P, 1], F32, name=f"shift{i}")
                    nc.vector.scalar_tensor_tensor(shift[:], mean, -1.0, one_rstd, ALU.mult, ALU.mult)
                    nc.scalar.activation(
                        normed[:, i, 2 * P :], turned[i][:], ACT.Identity, bias=shift[:], scale=one_rstd
                    )
                for b in range(BLOCKS):
                    nc.tensor.transpose(back[b][:, k * P : (k + 1) * P], normed[:, i, b * P : (b + 1) * P], identity[:])
            for b in range(BLOCKS):
                out_piece = held.tile([P, M], F32, name=f"out{t}_{b}")
                gain, bias = gain_bias[:, b : b + 1], gain_bias[:, BLOCKS + b : BLOCKS + b + 1]
                if t == HALVES - 1 and b % 2 == 1:
                    nc.vector.tensor_scalar(out_piece[:], back[b][:, :M], gain, bias, ALU.mult, ALU.add)
                else:
                    nc.scalar.activation(out_piece[:], back[b][:, :M], ACT.Identity, bias=bias, scale=gain)
                nc.sync.dma_start(out[b * P : (b + 1) * P, t * M : (t + 1) * M], out_piece[:])
